import numpy as np
import ml_dtypes


def mxq(x, axis, fmt="e4m3"):
    dtype, down = {"e4m3": (ml_dtypes.float8_e4m3fn, 7), "e5m2": (ml_dtypes.float8_e5m2, 14)}[fmt]
    v = np.moveaxis(np.asarray(x, np.float32).astype(ml_dtypes.bfloat16).astype(np.float64), axis, -1)
    blocks = v.reshape(v.shape[:-1] + (-1, 32))
    amax = np.abs(blocks).max(-1, keepdims=True)
    byte = np.maximum(np.where(amax > 0, np.frexp(amax)[1] - 1 + 127, 0) - down, 1)
    scale = np.exp2(byte - 127.0)
    codes = (blocks / scale).astype(np.float32).astype(dtype).astype(np.float64)
    return np.moveaxis((codes * scale).reshape(v.shape), -1, axis)


WIDE = False


def mx_kscale(k):
    if not WIDE:
        return np.ones(k)
    levels = np.array([10, -10, 5, -5, 0])
    a = np.random.permutation(np.resize(levels, k // 512 * 4)).reshape(k // 512, 4)
    idx = np.arange(k)
    return np.exp2(a[idx // 512, idx % 128 // 32])


BF16 = ml_dtypes.bfloat16


def bf(x):
    return np.asarray(x, np.float32).astype(BF16)


def f64(x):
    return np.asarray(x).astype(np.float64)


E2M1 = np.array([0.0, 0.5, 1.0, 1.5, 2.0, 3.0, 4.0, 6.0, -0.0, -0.5, -1.0, -1.5, -2.0, -3.0, -4.0, -6.0])


def pack_weight(w, fmt):
    k, n = w.shape
    w = f64(bf(w)).reshape(k // 32, 32, n)
    amax = np.abs(w).max(1)
    if fmt == "e4m3":
        byte = np.frexp(amax)[1] - 1 + 127 - 7
    else:
        mant, ex = np.frexp(amax / 6.0)
        byte = np.where(mant > 0.5, ex, ex - 1) + 127
    byte = np.clip(np.where(amax > 0, byte, 1), 1, 254)
    scaled = (w * np.exp2(127.0 - byte)[:, None, :]).reshape(k, n).astype(np.float32)
    by_word = np.ascontiguousarray(scaled.reshape(k // 512, 128, 4, n).transpose(0, 1, 3, 2))
    if fmt == "e4m3":
        words = by_word.astype(ml_dtypes.float8_e4m3fn).view(np.uint8)
    else:
        c = by_word.astype(ml_dtypes.float4_e2m1fn).view(np.uint8) & 0xF
        words = c[..., 0::2] | (c[..., 1::2] << 4)
    return np.ascontiguousarray(words), np.ascontiguousarray(byte.astype(np.uint8).reshape(k // 512, 16, n))


def unpack_weight(words, scales, fmt):
    g, p, n, _ = words.shape
    if fmt == "e4m3":
        vals = np.ascontiguousarray(words).view(ml_dtypes.float8_e4m3fn).astype(np.float64)
    else:
        nib = np.empty((g, p, n, 4), np.uint8)
        nib[..., 0::2] = words & 0xF
        nib[..., 1::2] = words >> 4
        vals = E2M1[nib]
    vals = vals * np.repeat(np.exp2(scales.astype(np.float64) - 127.0), 8, axis=1)[..., None]
    return vals.transpose(0, 1, 3, 2).reshape(g * 512, n)


S, H, E, P, C = 1024, 256, 416, 64, 32
IN0 = E + P + C + 4 * H
FMT = "e4m3"


def sigmoid(v):
    return 1.0 / (1.0 + np.exp(-v))


def lstm_gates(g, c):
    i, f, gg, o = np.split(g, 4, axis=-1)
    c2 = sigmoid(f) * c + sigmoid(i) * np.tanh(gg)
    return sigmoid(o) * np.tanh(c2)


def setup_inputs():
    n = np.random.standard_normal
    s = mx_kscale(IN0)
    a1, a2, a3, a4 = 2 * H, 4 * H, 4 * H + E, 4 * H + E + P
    d = {"hn_chunks": bf(n((S, 2 * H)) * s[:a1]), "hn_tags": bf(n((S, 2 * H)) * s[a1:a2]), "x": bf(n((S, E)) * s[a2:a3]),
         "tags": bf(n((S, P)) * s[a3:a4]), "chunks": bf(n((S, C)) * s[a4:]),
         "h0": bf(n((2, S, H))), "c0": bf(n((2, S, H)))}
    for k in ("f", "b"):
        words, scales = pack_weight(np.ascontiguousarray((n((4 * H, IN0)) / np.sqrt(IN0) / s).T), FMT)
        d["wih_" + k + "_words"] = words
        d["wih_" + k + "_scales"] = scales
        d["whh_" + k] = bf(n((4 * H, H)) * 0.7 / np.sqrt(H))
        d["bih_" + k] = bf(n(4 * H) * 0.2)
        d["bhh_" + k] = bf(n(4 * H) * 0.2)
    return d


def reference(hn_chunks, hn_tags, x, tags, chunks, h0, c0, wih_f_words, wih_f_scales, whh_f, bih_f, bhh_f, wih_b_words, wih_b_scales, whh_b, bih_b, bhh_b):
    gt = np.concatenate([f64(hn_chunks), f64(hn_tags), f64(x), f64(tags), f64(chunks)], axis=1)
    gq = mxq(gt, 1, "e4m3")
    gf = (gq @ unpack_weight(wih_f_words, wih_f_scales, FMT)) + f64(bih_f) + f64(h0)[0] @ f64(whh_f).T + f64(bhh_f)
    gb = (gq @ unpack_weight(wih_b_words, wih_b_scales, FMT)) + f64(bih_b) + f64(h0)[1] @ f64(whh_b).T + f64(bhh_b)
    return np.concatenate([lstm_gates(gf, f64(c0)[0]), lstm_gates(gb, f64(c0)[1])], axis=-1)

@@ -1,0 +1,276 @@
+from contextlib import ExitStack
+
+import concourse.mybir as mybir
+from concourse.masks import make_identity
+
+F32 = mybir.dt.float32
+BF16 = mybir.dt.bfloat16
+I32 = mybir.dt.int32
+U32 = mybir.dt.uint32
+U8 = mybir.dt.uint8
+FP8X4 = mybir.dt.float8_e4m3fn_x4
+ACT = mybir.ActivationFunctionType
+ALU = mybir.AluOpType
+
+P = 128
+TOKENS = 1024
+TILES = TOKENS // P
+H = 256
+GATES = 4 * H
+DIRS = 2
+K_PASS = 512
+PASSES = 3
+BANK = 512
+HALVES = GATES // BANK
+X_COLS, TAG_COLS, CHUNK_COLS = 416, 64, 32
+LOAD_TILES = 2
+PASS_GROUPS = ((0, 2), (2, 1))
+
+LEAD = 3
+
+FLOPS = 2 * TOKENS * (PASSES * K_PASS + H) * DIRS * GATES
+
+
+def tile_dependency_pa_kernel(
+    tc,
+    hn_chunks,
+    hn_tags,
+    x,
+    tags,
+    chunks,
+    h0,
+    c0,
+    wih_f_words,
+    wih_f_scales,
+    whh_f,
+    bih_f,
+    bhh_f,
+    wih_b_words,
+    wih_b_scales,
+    whh_b,
+    bih_b,
+    bhh_b,
+    out,
+):
+    nc = tc.nc
+    wih_words = (wih_f_words, wih_b_words)
+    wih_scales = (wih_f_scales, wih_b_scales)
+    whh = (whh_f, whh_b)
+    bih = (bih_f, bih_b)
+    bhh = (bhh_f, bhh_b)
+
+    def by_token(rows):
+        return rows.rearrange("(p m) c -> p m c", m=TILES)
+
+    def half(c):
+        return slice(c * BANK, (c + 1) * BANK)
+
+    with ExitStack() as ctx:
+        keep = ctx.enter_context(tc.tile_pool(name="keep", bufs=1))
+        work = ctx.enter_context(tc.tile_pool(name="work", bufs=3))
+        psum = ctx.enter_context(tc.psum_pool(name="psum", bufs=1))
+
+        def sum_bank():
+            bank = psum.tile([P, BANK], F32, tag="sums", bufs=5)
+            return bank
+
+        ctx.enter_context(tc.manual_schedule())
+
+        bias_rows = keep.tile([P, DIRS, GATES], BF16)
+        nc.vector.memset(bias_rows[:].bitcast(I32), 0)
+        w_planes = keep.tile([P, DIRS, GATES], U8, align_bytes=64)
+        nc.vector.memset(w_planes[:].bitcast(I32), 0)
+        ones = keep.tile([P, P], BF16)
+        nc.vector.memset(ones[:], 1.0)
+        ident = keep.tile([P, P], F32)
+        make_identity(nc, ident[:])
+
+        for d in range(DIRS):
+            nc.scalar.dma_start(out=bias_rows[0:1, d, :], in_=bih[d].rearrange("(o n) -> o n", o=1))
+            nc.scalar.dma_start(out=bias_rows[1:2, d, :], in_=bhh[d].rearrange("(o n) -> o n", o=1))
+        warm = keep.tile([P, 1], F32)
+        nc.vector.memset(warm[:], 0.0)
+        nc.scalar.activation(out=warm[:], in_=warm[:], func=ACT.Sigmoid)
+
+        whh_sb = keep.tile([P, DIRS, HALVES, BANK // P, H], BF16)
+        h0_sb = keep.tile([P, DIRS, TILES, H], BF16)
+        c0_sb = keep.tile([P, DIRS, TILES, H], BF16)
+        gt_sb = keep.tile([P, PASSES, TILES, K_PASS], BF16)
+        w_codes = keep.tile([P, DIRS, PASSES, GATES], U32, align_bytes=64)
+
+        def load_whh(d):
+            nc.sync.dma_start(
+                out=whh_sb[:, d, :, :, :], in_=whh[d].rearrange("(c p b) k -> p c b k", c=HALVES, p=P)
+            )
+
+        def load_h0(first):
+            some = slice(first, first + LOAD_TILES)
+            nc.sync.dma_start(
+                out=h0_sb[:, :, some, :], in_=h0.rearrange("d (p m) k -> p d m k", m=TILES)[:, :, some, :]
+            )
+
+        def load_gt(first):
+            some = slice(first, first + LOAD_TILES)
+            nc.sync.dma_start(out=gt_sb[:, 0, some, :], in_=by_token(hn_chunks)[:, some, :])
+            nc.sync.dma_start(out=gt_sb[:, 1, some, :], in_=by_token(hn_tags)[:, some, :])
+            nc.sync.dma_start(out=gt_sb[:, 2, some, 0:X_COLS], in_=by_token(x)[:, some, :])
+
+        def load_wih(d):
+            for quadrant in range(4):
+                nc.sync.dma_start(
+                    out=w_planes[32 * quadrant : 32 * quadrant + 4 * PASSES, d, :].bitcast(I32),
+                    in_=wih_scales[d][:, 4 * quadrant : 4 * quadrant + 4, :].bitcast(I32),
+                )
+            for g in range(PASSES):
+                nc.sync.dma_start(
+                    out=w_codes[:, d, g, :].bitcast(I32),
+                    in_=wih_words[d][g].rearrange("p n t -> p (n t)").bitcast(I32),
+                )
+
+        load_h0(0)
+        load_whh(0)
+        load_whh(1)
+        load_h0(LOAD_TILES)
+        nc.sync.dma_start(out=gt_sb[:, 2, :, X_COLS : X_COLS + TAG_COLS], in_=by_token(tags))
+        nc.sync.dma_start(out=gt_sb[:, 2, :, X_COLS + TAG_COLS : K_PASS], in_=by_token(chunks))
+        load_gt(0)
+        for first in range(2 * LOAD_TILES, TILES, LOAD_TILES):
+            load_h0(first)
+        load_wih(0)
+        load_gt(LOAD_TILES)
+        load_wih(1)
+        for d in range(DIRS):
+            nc.sync.dma_start(out=c0_sb[:, d, :, :], in_=by_token(c0[d]))
+        for first in range(2 * LOAD_TILES, TILES, LOAD_TILES):
+            load_gt(first)
+
+        bias = keep.tile([P, DIRS, GATES], F32)
+        whh_t = keep.tile([P, DIRS, GATES], F32)
+
+        def spread_bias(d):
+            for c in range(HALVES):
+                spread = sum_bank()
+                nc.tensor.matmul(out=spread[:], lhsT=ones[:], rhs=bias_rows[:, d, half(c)], start=True, stop=True)
+                nc.scalar.copy(out=bias[:, d, half(c)], in_=spread[:])
+
+        def transpose_whh(d):
+            for c in range(HALVES):
+                turned = sum_bank()
+                for b in range(BANK // P):
+                    nc.tensor.transpose(turned[:, b * P : (b + 1) * P], whh_sb[:, d, c, b, :].bitcast(F32), ident[:])
+                nc.vector.tensor_copy(
+                    out=whh_t[:, d, half(c)].rearrange("j (p b) -> j p b", p=P),
+                    in_=turned[:].rearrange("j (b p) -> j p b", p=P),
+                )
+
+        def transpose_h0(m):
+            turned = psum.tile([P, DIRS, P], F32, tag="turned_h0")
+            for d in range(DIRS):
+                nc.tensor.transpose(turned[:, d, :], h0_sb[:, d, m, :].bitcast(F32), ident[:])
+            h0_t = work.tile([P, DIRS, P], F32, tag="h0_t")
+            nc.scalar.copy(out=h0_t[:], in_=turned[:])
+            return h0_t
+
+        def transpose_gt(m):
+            grouped = work.tile([P, PASSES * P * 4], BF16, tag="grouped", align_bytes=64)
+            words = grouped[:].bitcast(F32).rearrange("p (g t u) -> p g t u", g=PASSES, u=2)
+            for first, count in PASS_GROUPS:
+                turned = psum.tile([P, count, 2, P], F32, tag="turned_gt%d" % first)
+                for g in range(count):
+                    for u in range(2):
+                        nc.tensor.transpose(
+                            turned[:, g, u, :], gt_sb[:, first + g, m, :].bitcast(F32)[:, u : K_PASS // 2 : 2], ident[:]
+                        )
+                nc.scalar.copy(out=words[:, first : first + count], in_=turned[:].rearrange("p g u t -> p g t u"))
+            return grouped
+
+        def quantise_gt(grouped):
+            codes = work.tile([P, PASSES * P], U32, tag="codes", align_bytes=64)
+            scales = work.tile([P, PASSES * P], U8, tag="scales", align_bytes=64)
+            for first, count in PASS_GROUPS:
+                cols = slice(first * P, (first + count) * P)
+                nc.vector.quantize_mx(
+                    out=codes[:, cols].bitcast(FP8X4),
+                    scales=scales[:, cols],
+                    in_=grouped[:, 4 * first * P : 4 * (first + count) * P],
+                )
+            return codes, scales
+
+        def hidden_product(h0_t, gates, d):
+            for c in range(HALVES):
+                sums = sum_bank()
+                for e in range(2):
+                    nc.tensor.matmul(
+                        out=sums[:],
+                        lhsT=h0_t[:, d, :].bitcast(BF16)[:, e : 2 * P : 2],
+                        rhs=whh_t[:, d, half(c)].bitcast(BF16)[:, e : 2 * BANK : 2],
+                        start=(e == 0),
+                        stop=(e == 1),
+                    )
+                nc.vector.tensor_tensor(out=gates[:, d, half(c)], in0=sums[:], in1=bias[:, d, half(c)], op=ALU.add)
+
+        def input_product(codes, scales, gates):
+            for c in range(HALVES):
+                for d in range(DIRS):
+                    sums = sum_bank()
+                    for g in range(PASSES):
+                        nc.tensor.matmul_mx(
+                            out=sums[:],
+                            lhsT=codes[:, g * P : (g + 1) * P].bitcast(FP8X4),
+                            lhsT_scale=scales[:, g * P : (g + 1) * P],
+                            rhs=w_codes[:, d, g, half(c)].bitcast(FP8X4),
+                            rhs_scale=w_planes[4 * g : P, d, half(c)],
+                            start=(g == 0),
+                            stop=(g == PASSES - 1),
+                        )
+                    nc.vector.tensor_tensor(out=gates[:, d, half(c)], in0=sums[:], in1=gates[:, d, half(c)], op=ALU.add)
+
+        def cell_keep(m, gates):
+            kept = work.tile([P, DIRS, H], F32, tag="kept")
+            nc.scalar.activation(out=gates[:, :, 0 : 2 * H], in_=gates[:, :, 0 : 2 * H], func=ACT.Sigmoid)
+            nc.gpsimd.tensor_tensor(out=kept[:], in0=gates[:, :, H : 2 * H], in1=c0_sb[:, :, m, :], op=ALU.mult)
+            return kept
+
+        def cell_update(m, gates, kept):
+            engine = nc.vector if m == TILES - 1 else nc.gpsimd
+            state = work.tile([P, DIRS, H], F32, tag="state")
+            nc.scalar.activation(out=gates[:, :, 2 * H : 3 * H], in_=gates[:, :, 2 * H : 3 * H], func=ACT.Tanh)
+            engine.tensor_tensor(out=state[:], in0=gates[:, :, 0:H], in1=gates[:, :, 2 * H : 3 * H], op=ALU.mult)
+            engine.tensor_tensor(out=state[:], in0=state[:], in1=kept[:], op=ALU.add)
+            nc.scalar.activation(out=gates[:, :, 3 * H : 4 * H], in_=gates[:, :, 3 * H : 4 * H], func=ACT.Sigmoid)
+            return state
+
+        def cell_output(m, gates, state):
+            hidden = work.tile([P, DIRS, H], F32, tag="hidden")
+            nc.scalar.activation(out=state[:], in_=state[:], func=ACT.Tanh)
+            nc.vector.tensor_tensor(out=hidden[:], in0=gates[:, :, 3 * H : 4 * H], in1=state[:], op=ALU.mult)
+            nc.sync.dma_start(out=by_token(out)[:, m, :], in_=hidden[:].rearrange("p d j -> p (d j)"))
+
+        h0_turned = {0: transpose_h0(0)}
+        gates_of = {}
+        grouped_of = {}
+        quantised = {}
+        state_of = {}
+        for r in range(TILES + LEAD + 1):
+            m = r - LEAD
+            if r + 1 < TILES:
+                h0_turned[r + 1] = transpose_h0(r + 1)
+            if 0 <= m + 2 < TILES:
+                grouped_of[m + 2] = transpose_gt(m + 2)
+            if 0 <= m + 1 < TILES:
+                quantised[m + 1] = quantise_gt(grouped_of[m + 1])
+            if r < TILES:
+                gates = work.tile([P, DIRS, GATES], F32, tag="gates", bufs=LEAD + 3)
+                gates_of[r] = gates
+                for d in range(DIRS):
+                    if r == 0:
+                        spread_bias(d)
+                        transpose_whh(d)
+                    hidden_product(h0_turned[r], gates, d)
+            if 0 <= m < TILES:
+                input_product(quantised[m][0], quantised[m][1], gates_of[m])
+                kept = cell_keep(m, gates_of[m])
+            if 0 <= m - 1:
+                cell_output(m - 1, gates_of[m - 1], state_of[m - 1])
+            if 0 <= m < TILES:
+                state_of[m] = cell_update(m, gates_of[m], kept)

@@ -23,10 +23,9 @@ PASSES = 3
 BANK = 512
 HALVES = GATES // BANK
 X_COLS, TAG_COLS, CHUNK_COLS = 416, 64, 32
-LOAD_TILES = 2
-PASS_GROUPS = ((0, 2), (2, 1))
-
-LEAD = 3
+PAIR = 2
+PAIRS = TILES // PAIR
+UNITS = DIRS * PAIRS
 
 FLOPS = 2 * TOKENS * (PASSES * K_PASS + H) * DIRS * GATES
 
@@ -65,13 +64,19 @@ def tile_dependency_pa_kernel(
     def half(c):
         return slice(c * BANK, (c + 1) * BANK)
 
+    def block(b):
+        return slice(b * P, (b + 1) * P)
+
+    def pair_tiles(j):
+        return slice(j * PAIR, (j + 1) * PAIR)
+
     with ExitStack() as ctx:
         keep = ctx.enter_context(tc.tile_pool(name="keep", bufs=1))
         work = ctx.enter_context(tc.tile_pool(name="work", bufs=3))
         psum = ctx.enter_context(tc.psum_pool(name="psum", bufs=1))
 
-        def sum_bank():
-            bank = psum.tile([P, BANK], F32, tag="sums", bufs=5)
+        def next_bank():
+            bank = psum.tile([P, BANK], F32, tag="bank", bufs=8)
             return bank
 
         ctx.enter_context(tc.manual_schedule())
@@ -85,9 +90,6 @@ def tile_dependency_pa_kernel(
         ident = keep.tile([P, P], F32)
         make_identity(nc, ident[:])
 
-        for d in range(DIRS):
-            nc.scalar.dma_start(out=bias_rows[0:1, d, :], in_=bih[d].rearrange("(o n) -> o n", o=1))
-            nc.scalar.dma_start(out=bias_rows[1:2, d, :], in_=bhh[d].rearrange("(o n) -> o n", o=1))
         warm = keep.tile([P, 1], F32)
         nc.vector.memset(warm[:], 0.0)
         nc.scalar.activation(out=warm[:], in_=warm[:], func=ACT.Sigmoid)
@@ -98,19 +100,16 @@ def tile_dependency_pa_kernel(
         gt_sb = keep.tile([P, PASSES, TILES, K_PASS], BF16)
         w_codes = keep.tile([P, DIRS, PASSES, GATES], U32, align_bytes=64)
 
-        def load_whh(d):
+        def load_hidden(d):
             nc.sync.dma_start(
                 out=whh_sb[:, d, :, :, :], in_=whh[d].rearrange("(c p b) k -> p c b k", c=HALVES, p=P)
             )
+            nc.sync.dma_start(out=h0_sb[:, d, :, :], in_=by_token(h0[d]))
+            nc.sync.dma_start(out=bias_rows[0:1, d, :], in_=bih[d].rearrange("(o n) -> o n", o=1))
+            nc.sync.dma_start(out=bias_rows[1:2, d, :], in_=bhh[d].rearrange("(o n) -> o n", o=1))
 
-        def load_h0(first):
-            some = slice(first, first + LOAD_TILES)
-            nc.sync.dma_start(
-                out=h0_sb[:, :, some, :], in_=h0.rearrange("d (p m) k -> p d m k", m=TILES)[:, :, some, :]
-            )
-
-        def load_gt(first):
-            some = slice(first, first + LOAD_TILES)
+        def load_gt(j):
+            some = pair_tiles(j)
             nc.sync.dma_start(out=gt_sb[:, 0, some, :], in_=by_token(hn_chunks)[:, some, :])
             nc.sync.dma_start(out=gt_sb[:, 1, some, :], in_=by_token(hn_tags)[:, some, :])
             nc.sync.dma_start(out=gt_sb[:, 2, some, 0:X_COLS], in_=by_token(x)[:, some, :])
@@ -127,150 +126,158 @@ def tile_dependency_pa_kernel(
                     in_=wih_words[d][g].rearrange("p n t -> p (n t)").bitcast(I32),
                 )
 
-        load_h0(0)
-        load_whh(0)
-        load_whh(1)
-        load_h0(LOAD_TILES)
+        def load_c0(d):
+            nc.sync.dma_start(out=c0_sb[:, d, :, :], in_=by_token(c0[d]))
+
+        load_hidden(0)
         nc.sync.dma_start(out=gt_sb[:, 2, :, X_COLS : X_COLS + TAG_COLS], in_=by_token(tags))
         nc.sync.dma_start(out=gt_sb[:, 2, :, X_COLS + TAG_COLS : K_PASS], in_=by_token(chunks))
         load_gt(0)
-        for first in range(2 * LOAD_TILES, TILES, LOAD_TILES):
-            load_h0(first)
+        load_gt(1)
         load_wih(0)
-        load_gt(LOAD_TILES)
+        load_c0(0)
+        load_gt(2)
+        load_gt(3)
+        load_hidden(1)
         load_wih(1)
-        for d in range(DIRS):
-            nc.sync.dma_start(out=c0_sb[:, d, :, :], in_=by_token(c0[d]))
-        for first in range(2 * LOAD_TILES, TILES, LOAD_TILES):
-            load_gt(first)
+        load_c0(1)
 
         bias = keep.tile([P, DIRS, GATES], F32)
         whh_t = keep.tile([P, DIRS, GATES], F32)
+        h0_t = keep.tile([P, DIRS, TILES * P], F32)
 
         def spread_bias(d):
             for c in range(HALVES):
-                spread = sum_bank()
+                spread = next_bank()
                 nc.tensor.matmul(out=spread[:], lhsT=ones[:], rhs=bias_rows[:, d, half(c)], start=True, stop=True)
                 nc.scalar.copy(out=bias[:, d, half(c)], in_=spread[:])
 
         def transpose_whh(d):
             for c in range(HALVES):
-                turned = sum_bank()
+                turned = next_bank()
                 for b in range(BANK // P):
-                    nc.tensor.transpose(turned[:, b * P : (b + 1) * P], whh_sb[:, d, c, b, :].bitcast(F32), ident[:])
+                    nc.tensor.transpose(turned[:, block(b)], whh_sb[:, d, c, b, :].bitcast(F32), ident[:])
                 nc.vector.tensor_copy(
                     out=whh_t[:, d, half(c)].rearrange("j (p b) -> j p b", p=P),
                     in_=turned[:].rearrange("j (b p) -> j p b", p=P),
                 )
 
-        def transpose_h0(m):
-            turned = psum.tile([P, DIRS, P], F32, tag="turned_h0")
-            for d in range(DIRS):
-                nc.tensor.transpose(turned[:, d, :], h0_sb[:, d, m, :].bitcast(F32), ident[:])
-            h0_t = work.tile([P, DIRS, P], F32, tag="h0_t")
-            nc.scalar.copy(out=h0_t[:], in_=turned[:])
-            return h0_t
+        def transpose_h0(d):
+            for c in range(TILES * P // BANK):
+                turned = next_bank()
+                for b in range(BANK // P):
+                    nc.tensor.transpose(turned[:, block(b)], h0_sb[:, d, c * (BANK // P) + b, :].bitcast(F32), ident[:])
+                nc.scalar.copy(out=h0_t[:, d, half(c)], in_=turned[:])
 
-        def transpose_gt(m):
-            grouped = work.tile([P, PASSES * P * 4], BF16, tag="grouped", align_bytes=64)
-            words = grouped[:].bitcast(F32).rearrange("p (g t u) -> p g t u", g=PASSES, u=2)
-            for first, count in PASS_GROUPS:
-                turned = psum.tile([P, count, 2, P], F32, tag="turned_gt%d" % first)
-                for g in range(count):
-                    for u in range(2):
+        gt_codes = keep.tile([P, PASSES, TILES * P], U32, align_bytes=64)
+        gt_scales = keep.tile([P, PASSES, TILES * P], U8, align_bytes=64)
+
+        def transpose_gt(j):
+            grouped = work.tile([P, PASSES, PAIR * P * 4], BF16, tag="grouped", align_bytes=64)
+            for g in range(PASSES):
+                turned = next_bank()
+                for t in range(PAIR):
+                    for w in range(2):
                         nc.tensor.transpose(
-                            turned[:, g, u, :], gt_sb[:, first + g, m, :].bitcast(F32)[:, u : K_PASS // 2 : 2], ident[:]
+                            turned[:, block(2 * t + w)],
+                            gt_sb[:, g, j * PAIR + t, :].bitcast(F32)[:, w : K_PASS // 2 : 2],
+                            ident[:],
                         )
-                nc.scalar.copy(out=words[:, first : first + count], in_=turned[:].rearrange("p g u t -> p g t u"))
+                nc.scalar.copy(
+                    out=grouped[:, g, :].bitcast(F32).rearrange("p (t c w) -> p t c w", t=PAIR, w=2),
+                    in_=turned[:].rearrange("p (t w c) -> p t c w", t=PAIR, w=2),
+                )
             return grouped
 
-        def quantise_gt(grouped):
-            codes = work.tile([P, PASSES * P], U32, tag="codes", align_bytes=64)
-            scales = work.tile([P, PASSES * P], U8, tag="scales", align_bytes=64)
-            for first, count in PASS_GROUPS:
-                cols = slice(first * P, (first + count) * P)
+        def quantise_gt(j, grouped):
+            cols = slice(j * PAIR * P, (j + 1) * PAIR * P)
+            for g in range(PASSES):
                 nc.vector.quantize_mx(
-                    out=codes[:, cols].bitcast(FP8X4),
-                    scales=scales[:, cols],
-                    in_=grouped[:, 4 * first * P : 4 * (first + count) * P],
+                    out=gt_codes[:, g, cols].bitcast(FP8X4), scales=gt_scales[:, g, cols], in_=grouped[:, g, :]
                 )
-            return codes, scales
 
-        def hidden_product(h0_t, gates, d):
-            for c in range(HALVES):
-                sums = sum_bank()
-                for e in range(2):
-                    nc.tensor.matmul(
-                        out=sums[:],
-                        lhsT=h0_t[:, d, :].bitcast(BF16)[:, e : 2 * P : 2],
-                        rhs=whh_t[:, d, half(c)].bitcast(BF16)[:, e : 2 * BANK : 2],
-                        start=(e == 0),
-                        stop=(e == 1),
-                    )
-                nc.vector.tensor_tensor(out=gates[:, d, half(c)], in0=sums[:], in1=bias[:, d, half(c)], op=ALU.add)
+        def hidden_product(d, j):
+            gates = work.tile([P, PAIR, GATES], F32, tag="gates", bufs=4)
+            for t in range(PAIR):
+                for c in range(HALVES):
+                    sums = next_bank()
+                    for e in range(2):
+                        nc.tensor.matmul(
+                            out=sums[:],
+                            lhsT=h0_t[:, d, block(j * PAIR + t)].bitcast(BF16)[:, e : 2 * P : 2],
+                            rhs=whh_t[:, d, half(c)].bitcast(BF16)[:, e : 2 * BANK : 2],
+                            start=(e == 0),
+                            stop=(e == 1),
+                        )
+                    nc.vector.tensor_tensor(out=gates[:, t, half(c)], in0=sums[:], in1=bias[:, d, half(c)], op=ALU.add)
+            return gates
 
-        def input_product(codes, scales, gates):
+        def input_product(d, j, gates):
             for c in range(HALVES):
-                for d in range(DIRS):
-                    sums = sum_bank()
+                for t in range(PAIR):
+                    sums = next_bank()
                     for g in range(PASSES):
                         nc.tensor.matmul_mx(
                             out=sums[:],
-                            lhsT=codes[:, g * P : (g + 1) * P].bitcast(FP8X4),
-                            lhsT_scale=scales[:, g * P : (g + 1) * P],
+                            lhsT=gt_codes[:, g, block(j * PAIR + t)].bitcast(FP8X4),
+                            lhsT_scale=gt_scales[:, g, block(j * PAIR + t)],
                             rhs=w_codes[:, d, g, half(c)].bitcast(FP8X4),
                             rhs_scale=w_planes[4 * g : P, d, half(c)],
                             start=(g == 0),
                             stop=(g == PASSES - 1),
                         )
-                    nc.vector.tensor_tensor(out=gates[:, d, half(c)], in0=sums[:], in1=gates[:, d, half(c)], op=ALU.add)
+                    nc.vector.tensor_tensor(out=gates[:, t, half(c)], in0=sums[:], in1=gates[:, t, half(c)], op=ALU.add)
 
-        def cell_keep(m, gates):
-            kept = work.tile([P, DIRS, H], F32, tag="kept")
+        def cell_engine(u):
+            return nc.vector if u == UNITS - 1 else nc.gpsimd
+
+        def cell_keep(u, gates):
+            d, j = divmod(u, PAIRS)
+            kept = work.tile([P, PAIR, H], F32, tag="kept")
             nc.scalar.activation(out=gates[:, :, 0 : 2 * H], in_=gates[:, :, 0 : 2 * H], func=ACT.Sigmoid)
-            nc.gpsimd.tensor_tensor(out=kept[:], in0=gates[:, :, H : 2 * H], in1=c0_sb[:, :, m, :], op=ALU.mult)
+            cell_engine(u).tensor_tensor(
+                out=kept[:], in0=gates[:, :, H : 2 * H], in1=c0_sb[:, d, pair_tiles(j), :], op=ALU.mult
+            )
             return kept
 
-        def cell_update(m, gates, kept):
-            engine = nc.vector if m == TILES - 1 else nc.gpsimd
-            state = work.tile([P, DIRS, H], F32, tag="state")
+        def cell_update(u, gates, kept):
+            state = work.tile([P, PAIR, H], F32, tag="state")
             nc.scalar.activation(out=gates[:, :, 2 * H : 3 * H], in_=gates[:, :, 2 * H : 3 * H], func=ACT.Tanh)
-            engine.tensor_tensor(out=state[:], in0=gates[:, :, 0:H], in1=gates[:, :, 2 * H : 3 * H], op=ALU.mult)
-            engine.tensor_tensor(out=state[:], in0=state[:], in1=kept[:], op=ALU.add)
+            cell_engine(u).tensor_tensor(
+                out=state[:], in0=gates[:, :, 0:H], in1=gates[:, :, 2 * H : 3 * H], op=ALU.mult
+            )
+            cell_engine(u).tensor_tensor(out=state[:], in0=state[:], in1=kept[:], op=ALU.add)
             nc.scalar.activation(out=gates[:, :, 3 * H : 4 * H], in_=gates[:, :, 3 * H : 4 * H], func=ACT.Sigmoid)
             return state
 
-        def cell_output(m, gates, state):
-            hidden = work.tile([P, DIRS, H], F32, tag="hidden")
+        def cell_output(u, gates, state):
+            d, j = divmod(u, PAIRS)
+            hidden = work.tile([P, PAIR, H], F32, tag="hidden")
             nc.scalar.activation(out=state[:], in_=state[:], func=ACT.Tanh)
-            nc.vector.tensor_tensor(out=hidden[:], in0=gates[:, :, 3 * H : 4 * H], in1=state[:], op=ALU.mult)
-            nc.sync.dma_start(out=by_token(out)[:, m, :], in_=hidden[:].rearrange("p d j -> p (d j)"))
+            cell_engine(u).tensor_tensor(out=hidden[:], in0=gates[:, :, 3 * H : 4 * H], in1=state[:], op=ALU.mult)
+            nc.sync.dma_start(out=by_token(out)[:, pair_tiles(j), d * H : (d + 1) * H], in_=hidden[:])
 
-        h0_turned = {0: transpose_h0(0)}
+        def prepare(d):
+            transpose_whh(d)
+            transpose_h0(d)
+            spread_bias(d)
+
+        prepare(0)
         gates_of = {}
         grouped_of = {}
-        quantised = {}
         state_of = {}
-        for r in range(TILES + LEAD + 1):
-            m = r - LEAD
-            if r + 1 < TILES:
-                h0_turned[r + 1] = transpose_h0(r + 1)
-            if 0 <= m + 2 < TILES:
-                grouped_of[m + 2] = transpose_gt(m + 2)
-            if 0 <= m + 1 < TILES:
-                quantised[m + 1] = quantise_gt(grouped_of[m + 1])
-            if r < TILES:
-                gates = work.tile([P, DIRS, GATES], F32, tag="gates", bufs=LEAD + 3)
-                gates_of[r] = gates
-                for d in range(DIRS):
-                    if r == 0:
-                        spread_bias(d)
-                        transpose_whh(d)
-                    hidden_product(h0_turned[r], gates, d)
-            if 0 <= m < TILES:
-                input_product(quantised[m][0], quantised[m][1], gates_of[m])
-                kept = cell_keep(m, gates_of[m])
-            if 0 <= m - 1:
-                cell_output(m - 1, gates_of[m - 1], state_of[m - 1])
-            if 0 <= m < TILES:
-                state_of[m] = cell_update(m, gates_of[m], kept)
+        for u in range(UNITS + 2):
+            if u == PAIRS - 1:
+                prepare(1)
+            if 0 <= u - 1 < PAIRS:
+                quantise_gt(u - 1, grouped_of[u - 1])
+            if u < UNITS:
+                gates_of[u] = hidden_product(u // PAIRS, u % PAIRS)
+            if u < PAIRS:
+                grouped_of[u] = transpose_gt(u)
+            if 0 <= u - 1 < UNITS:
+                input_product((u - 1) // PAIRS, (u - 1) % PAIRS, gates_of[u - 1])
+                kept = cell_keep(u - 1, gates_of[u - 1])
+                state_of[u - 1] = cell_update(u - 1, gates_of[u - 1], kept)
+            if 0 <= u - 2:
+                cell_output(u - 2, gates_of[u - 2], state_of[u - 2])

@@ -172,17 +172,22 @@ def tile_dependency_pa_kernel(
         gt_codes = keep.tile([P, PASSES, TILES * P], U32, align_bytes=64)
         gt_scales = keep.tile([P, PASSES, TILES * P], U8, align_bytes=64)
 
-        def transpose_gt(j):
+        def sort_gt(j):
+            halves = work.tile([P, PASSES, PAIR, 2, P], F32, tag="halves")
+            for g in range(PASSES):
+                nc.scalar.copy(
+                    out=halves[:, g, :, :, :],
+                    in_=gt_sb[:, g, pair_tiles(j), :].bitcast(F32).rearrange("p t (c w) -> p t w c", w=2),
+                )
+            return halves
+
+        def transpose_gt(halves):
             grouped = work.tile([P, PASSES, PAIR * P * 4], BF16, tag="grouped", align_bytes=64)
             for g in range(PASSES):
                 turned = next_bank()
                 for t in range(PAIR):
                     for w in range(2):
-                        nc.tensor.transpose(
-                            turned[:, block(2 * t + w)],
-                            gt_sb[:, g, j * PAIR + t, :].bitcast(F32)[:, w : K_PASS // 2 : 2],
-                            ident[:],
-                        )
+                        nc.tensor.transpose(turned[:, block(2 * t + w)], halves[:, g, t, w, :], ident[:])
                 nc.scalar.copy(
                     out=grouped[:, g, :].bitcast(F32).rearrange("p (t c w) -> p t c w", t=PAIR, w=2),
                     in_=turned[:].rearrange("p (t w c) -> p t c w", t=PAIR, w=2),
@@ -263,6 +268,7 @@ def tile_dependency_pa_kernel(
             spread_bias(d)
 
         prepare(0)
+        sorted_of = {0: sort_gt(0)}
         gates_of = {}
         grouped_of = {}
         state_of = {}
@@ -274,7 +280,9 @@ def tile_dependency_pa_kernel(
             if u < UNITS:
                 gates_of[u] = hidden_product(u // PAIRS, u % PAIRS)
             if u < PAIRS:
-                grouped_of[u] = transpose_gt(u)
+                grouped_of[u] = transpose_gt(sorted_of[u])
+            if u + 1 < PAIRS:
+                sorted_of[u + 1] = sort_gt(u + 1)
             if 0 <= u - 1 < UNITS:
                 input_product((u - 1) // PAIRS, (u - 1) % PAIRS, gates_of[u - 1])
                 kept = cell_keep(u - 1, gates_of[u - 1])

@@ -217,50 +217,79 @@ def tile_dependency_pa_kernel(
                     nc.vector.tensor_tensor(out=gates[:, t, half(c)], in0=sums[:], in1=bias[:, d, half(c)], op=ALU.add)
             return gates
 
+        def input_columns(d, j, gates, t, cols):
+            sums = next_bank()
+            width = cols.stop - cols.start
+            for g in range(PASSES):
+                nc.tensor.matmul_mx(
+                    out=sums[:, 0:width],
+                    lhsT=gt_codes[:, g, block(j * PAIR + t)].bitcast(FP8X4),
+                    lhsT_scale=gt_scales[:, g, block(j * PAIR + t)],
+                    rhs=w_codes[:, d, g, cols].bitcast(FP8X4),
+                    rhs_scale=w_planes[4 * g : P, d, cols],
+                    start=(g == 0),
+                    stop=(g == PASSES - 1),
+                )
+            nc.vector.tensor_tensor(out=gates[:, t, cols], in0=sums[:, 0:width], in1=gates[:, t, cols], op=ALU.add)
+
         def input_product(d, j, gates):
             for c in range(HALVES):
                 for t in range(PAIR):
-                    sums = next_bank()
-                    for g in range(PASSES):
-                        nc.tensor.matmul_mx(
-                            out=sums[:],
-                            lhsT=gt_codes[:, g, block(j * PAIR + t)].bitcast(FP8X4),
-                            lhsT_scale=gt_scales[:, g, block(j * PAIR + t)],
-                            rhs=w_codes[:, d, g, half(c)].bitcast(FP8X4),
-                            rhs_scale=w_planes[4 * g : P, d, half(c)],
-                            start=(g == 0),
-                            stop=(g == PASSES - 1),
-                        )
-                    nc.vector.tensor_tensor(out=gates[:, t, half(c)], in0=sums[:], in1=gates[:, t, half(c)], op=ALU.add)
+                    input_columns(d, j, gates, t, half(c))
 
-        def cell_engine(u):
-            return nc.vector if u == UNITS - 1 else nc.gpsimd
+        def gate(gates, some, q, func):
+            nc.scalar.activation(
+                out=gates[:, some, q.start * H : q.stop * H], in_=gates[:, some, q.start * H : q.stop * H], func=func
+            )
 
-        def cell_keep(u, gates):
+        def count(some):
+            return some.stop - some.start
+
+        def keep_old(engine, u, gates, some):
             d, j = divmod(u, PAIRS)
-            kept = work.tile([P, PAIR, H], F32, tag="kept")
-            nc.scalar.activation(out=gates[:, :, 0 : 2 * H], in_=gates[:, :, 0 : 2 * H], func=ACT.Sigmoid)
-            cell_engine(u).tensor_tensor(
-                out=kept[:], in0=gates[:, :, H : 2 * H], in1=c0_sb[:, d, pair_tiles(j), :], op=ALU.mult
+            kept = work.tile([P, count(some), H], F32, tag="kept", bufs=4)
+            engine.tensor_tensor(
+                out=kept[:],
+                in0=gates[:, some, H : 2 * H],
+                in1=c0_sb[:, d, j * PAIR + some.start : j * PAIR + some.stop, :],
+                op=ALU.mult,
             )
             return kept
 
-        def cell_update(u, gates, kept):
-            state = work.tile([P, PAIR, H], F32, tag="state")
-            nc.scalar.activation(out=gates[:, :, 2 * H : 3 * H], in_=gates[:, :, 2 * H : 3 * H], func=ACT.Tanh)
-            cell_engine(u).tensor_tensor(
-                out=state[:], in0=gates[:, :, 0:H], in1=gates[:, :, 2 * H : 3 * H], op=ALU.mult
-            )
-            cell_engine(u).tensor_tensor(out=state[:], in0=state[:], in1=kept[:], op=ALU.add)
-            nc.scalar.activation(out=gates[:, :, 3 * H : 4 * H], in_=gates[:, :, 3 * H : 4 * H], func=ACT.Sigmoid)
+        def take_new(engine, gates, some):
+            state = work.tile([P, count(some), H], F32, tag="state", bufs=4)
+            engine.tensor_tensor(out=state[:], in0=gates[:, some, 0:H], in1=gates[:, some, 2 * H : 3 * H], op=ALU.mult)
             return state
 
-        def cell_output(u, gates, state):
-            d, j = divmod(u, PAIRS)
-            hidden = work.tile([P, PAIR, H], F32, tag="hidden")
+        def join(engine, state, kept):
+            engine.tensor_tensor(out=state[:], in0=state[:], in1=kept[:], op=ALU.add)
+
+        def squash(state):
             nc.scalar.activation(out=state[:], in_=state[:], func=ACT.Tanh)
-            cell_engine(u).tensor_tensor(out=hidden[:], in0=gates[:, :, 3 * H : 4 * H], in1=state[:], op=ALU.mult)
-            nc.sync.dma_start(out=by_token(out)[:, pair_tiles(j), d * H : (d + 1) * H], in_=hidden[:])
+
+        def emit(engine, u, gates, some, state):
+            d, j = divmod(u, PAIRS)
+            hidden = work.tile([P, count(some), H], F32, tag="hidden", bufs=4)
+            engine.tensor_tensor(out=hidden[:], in0=gates[:, some, 3 * H : 4 * H], in1=state[:], op=ALU.mult)
+            nc.sync.dma_start(
+                out=by_token(out)[:, j * PAIR + some.start : j * PAIR + some.stop, d * H : (d + 1) * H], in_=hidden[:]
+            )
+
+        I_F, GG, O = slice(0, 2), slice(2, 3), slice(3, 4)
+        BOTH, FIRST, SECOND = slice(0, 2), slice(0, 1), slice(1, 2)
+
+        def cell_start(u, gates):
+            gate(gates, BOTH, I_F, ACT.Sigmoid)
+            kept = keep_old(nc.gpsimd, u, gates, BOTH)
+            gate(gates, BOTH, GG, ACT.Tanh)
+            state = take_new(nc.gpsimd, gates, BOTH)
+            join(nc.gpsimd, state, kept)
+            gate(gates, BOTH, O, ACT.Sigmoid)
+            return state
+
+        def cell_end(u, gates, state):
+            squash(state)
+            emit(nc.gpsimd, u, gates, BOTH, state)
 
         def prepare(d):
             transpose_whh(d)
@@ -272,20 +301,47 @@ def tile_dependency_pa_kernel(
         gates_of = {}
         grouped_of = {}
         state_of = {}
-        for u in range(UNITS + 2):
+        for u in range(UNITS - 1):
             if u == PAIRS - 1:
                 prepare(1)
             if 0 <= u - 1 < PAIRS:
                 quantise_gt(u - 1, grouped_of[u - 1])
-            if u < UNITS:
-                gates_of[u] = hidden_product(u // PAIRS, u % PAIRS)
+            gates_of[u] = hidden_product(u // PAIRS, u % PAIRS)
             if u < PAIRS:
                 grouped_of[u] = transpose_gt(sorted_of[u])
             if u + 1 < PAIRS:
                 sorted_of[u + 1] = sort_gt(u + 1)
-            if 0 <= u - 1 < UNITS:
+            if 0 <= u - 1:
                 input_product((u - 1) // PAIRS, (u - 1) % PAIRS, gates_of[u - 1])
-                kept = cell_keep(u - 1, gates_of[u - 1])
-                state_of[u - 1] = cell_update(u - 1, gates_of[u - 1], kept)
+                state_of[u - 1] = cell_start(u - 1, gates_of[u - 1])
             if 0 <= u - 2:
-                cell_output(u - 2, gates_of[u - 2], state_of[u - 2])
+                cell_end(u - 2, gates_of[u - 2], state_of[u - 2])
+
+        last = UNITS - 1
+        d_last, j_last = divmod(last, PAIRS)
+        input_product(d_last, j_last - 1, gates_of[last - 1])
+        state_of[last - 1] = cell_start(last - 1, gates_of[last - 1])
+        cell_end(last - 2, gates_of[last - 2], state_of[last - 2])
+        gates = hidden_product(d_last, j_last)
+        input_columns(d_last, j_last, gates, 0, half(0))
+        input_columns(d_last, j_last, gates, 0, half(1))
+        input_columns(d_last, j_last, gates, 1, half(0))
+        input_columns(d_last, j_last, gates, 1, slice(2 * H, 3 * H))
+        input_columns(d_last, j_last, gates, 1, slice(3 * H, 4 * H))
+        gate(gates, FIRST, I_F, ACT.Sigmoid)
+        gate(gates, FIRST, GG, ACT.Tanh)
+        gate(gates, FIRST, O, ACT.Sigmoid)
+        gate(gates, SECOND, I_F, ACT.Sigmoid)
+        gate(gates, SECOND, GG, ACT.Tanh)
+        kept_first = keep_old(nc.vector, last, gates, FIRST)
+        state_first = take_new(nc.vector, gates, FIRST)
+        join(nc.vector, state_first, kept_first)
+        cell_end(last - 1, gates_of[last - 1], state_of[last - 1])
+        squash(state_first)
+        kept_second = keep_old(nc.vector, last, gates, SECOND)
+        state_second = take_new(nc.vector, gates, SECOND)
+        join(nc.vector, state_second, kept_second)
+        gate(gates, SECOND, O, ACT.Sigmoid)
+        emit(nc.vector, last, gates, FIRST, state_first)
+        squash(state_second)
+        emit(nc.vector, last, gates, SECOND, state_second)

@@ -202,7 +202,7 @@ def tile_dependency_pa_kernel(
                 )
 
         def hidden_product(d, j):
-            gates = work.tile([P, PAIR, GATES], F32, tag="gates", bufs=4)
+            gates = work.tile([P, PAIR, GATES], F32, tag="gates", bufs=5)
             for t in range(PAIR):
                 for c in range(HALVES):
                     sums = next_bank()
@@ -301,12 +301,16 @@ def tile_dependency_pa_kernel(
         gates_of = {}
         grouped_of = {}
         state_of = {}
+        gates_of[0] = hidden_product(0, 0)
         for u in range(UNITS - 1):
             if u == PAIRS - 1:
                 prepare(1)
             if 0 <= u - 1 < PAIRS:
                 quantise_gt(u - 1, grouped_of[u - 1])
-            gates_of[u] = hidden_product(u // PAIRS, u % PAIRS)
+            if u + 1 < PAIRS:
+                gates_of[u + 1] = hidden_product(0, u + 1)
+            if PAIRS <= u:
+                gates_of[u] = hidden_product(u // PAIRS, u % PAIRS)
             if u < PAIRS:
                 grouped_of[u] = transpose_gt(sorted_of[u])
             if u + 1 < PAIRS:
@@ -319,9 +323,14 @@ def tile_dependency_pa_kernel(
 
         last = UNITS - 1
         d_last, j_last = divmod(last, PAIRS)
-        input_product(d_last, j_last - 1, gates_of[last - 1])
-        state_of[last - 1] = cell_start(last - 1, gates_of[last - 1])
-        cell_end(last - 2, gates_of[last - 2], state_of[last - 2])
+        before = gates_of[last - 1]
+        input_product(d_last, j_last - 1, before)
+        squash(state_of[last - 2])
+        gate(before, BOTH, I_F, ACT.Sigmoid)
+        kept_before = keep_old(nc.gpsimd, last - 1, before, BOTH)
+        gate(before, BOTH, GG, ACT.Tanh)
+        state_before = take_new(nc.gpsimd, before, BOTH)
+        gate(before, BOTH, O, ACT.Sigmoid)
         gates = hidden_product(d_last, j_last)
         input_columns(d_last, j_last, gates, 0, half(0))
         input_columns(d_last, j_last, gates, 0, half(1))
@@ -333,15 +342,18 @@ def tile_dependency_pa_kernel(
         gate(gates, FIRST, O, ACT.Sigmoid)
         gate(gates, SECOND, I_F, ACT.Sigmoid)
         gate(gates, SECOND, GG, ACT.Tanh)
+        emit(nc.vector, last - 2, gates_of[last - 2], BOTH, state_of[last - 2])
+        join(nc.vector, state_before, kept_before)
+        squash(state_before)
         kept_first = keep_old(nc.vector, last, gates, FIRST)
         state_first = take_new(nc.vector, gates, FIRST)
         join(nc.vector, state_first, kept_first)
-        cell_end(last - 1, gates_of[last - 1], state_of[last - 1])
         squash(state_first)
         kept_second = keep_old(nc.vector, last, gates, SECOND)
         state_second = take_new(nc.vector, gates, SECOND)
         join(nc.vector, state_second, kept_second)
         gate(gates, SECOND, O, ACT.Sigmoid)
-        emit(nc.vector, last, gates, FIRST, state_first)
         squash(state_second)
+        emit(nc.vector, last - 1, before, BOTH, state_before)
+        emit(nc.vector, last, gates, FIRST, state_first)
         emit(nc.vector, last, gates, SECOND, state_second)

@@ -26,6 +26,7 @@ X_COLS, TAG_COLS, CHUNK_COLS = 416, 64, 32
 PAIR = 2
 PAIRS = TILES // PAIR
 UNITS = DIRS * PAIRS
+WARM_UP = 20
 
 FLOPS = 2 * TOKENS * (PASSES * K_PASS + H) * DIRS * GATES
 
@@ -81,12 +82,15 @@ def tile_dependency_pa_kernel(
 
         ctx.enter_context(tc.manual_schedule())
 
+        ones = keep.tile([P, P], BF16)
+        nc.vector.memset(ones[:], 1.0)
+        idle_sums = next_bank()
+        for n in range(WARM_UP):
+            nc.tensor.matmul(out=idle_sums[:, 0:P], lhsT=ones[:], rhs=ones[:], start=True, stop=True)
         bias_rows = keep.tile([P, DIRS, GATES], BF16)
         nc.vector.memset(bias_rows[:].bitcast(I32), 0)
         w_planes = keep.tile([P, DIRS, GATES], U8, align_bytes=64)
         nc.vector.memset(w_planes[:].bitcast(I32), 0)
-        ones = keep.tile([P, P], BF16)
-        nc.vector.memset(ones[:], 1.0)
         ident = keep.tile([P, P], F32)
         make_identity(nc, ident[:])
 
@@ -325,12 +329,12 @@ def tile_dependency_pa_kernel(
         d_last, j_last = divmod(last, PAIRS)
         before = gates_of[last - 1]
         input_product(d_last, j_last - 1, before)
-        squash(state_of[last - 2])
         gate(before, BOTH, I_F, ACT.Sigmoid)
         kept_before = keep_old(nc.gpsimd, last - 1, before, BOTH)
         gate(before, BOTH, GG, ACT.Tanh)
         state_before = take_new(nc.gpsimd, before, BOTH)
         gate(before, BOTH, O, ACT.Sigmoid)
+        squash(state_of[last - 2])
         gates = hidden_product(d_last, j_last)
         input_columns(d_last, j_last, gates, 0, half(0))
         input_columns(d_last, j_last, gates, 0, half(1))

from contextlib import ExitStack

import concourse.mybir as mybir
from concourse.masks import make_identity

F32 = mybir.dt.float32
BF16 = mybir.dt.bfloat16
I32 = mybir.dt.int32
U32 = mybir.dt.uint32
U8 = mybir.dt.uint8
FP8X4 = mybir.dt.float8_e4m3fn_x4
ACT = mybir.ActivationFunctionType
ALU = mybir.AluOpType

P = 128
TOKENS = 1024
TILES = TOKENS // P
H = 256
GATES = 4 * H
DIRS = 2
K_PASS = 512
PASSES = 3
BANK = 512
HALVES = GATES // BANK
X_COLS, TAG_COLS, CHUNK_COLS = 416, 64, 32
PAIR = 2
PAIRS = TILES // PAIR
UNITS = DIRS * PAIRS
WARM_UP = 20

FLOPS = 2 * TOKENS * (PASSES * K_PASS + H) * DIRS * GATES


def tile_dependency_pa_kernel(
    tc,
    hn_chunks,
    hn_tags,
    x,
    tags,
    chunks,
    h0,
    c0,
    wih_f_words,
    wih_f_scales,
    whh_f,
    bih_f,
    bhh_f,
    wih_b_words,
    wih_b_scales,
    whh_b,
    bih_b,
    bhh_b,
    out,
):
    nc = tc.nc
    wih_words = (wih_f_words, wih_b_words)
    wih_scales = (wih_f_scales, wih_b_scales)
    whh = (whh_f, whh_b)
    bih = (bih_f, bih_b)
    bhh = (bhh_f, bhh_b)

    def by_token(rows):
        return rows.rearrange("(p m) c -> p m c", m=TILES)

    def half(c):
        return slice(c * BANK, (c + 1) * BANK)

    def block(b):
        return slice(b * P, (b + 1) * P)

    def pair_tiles(j):
        return slice(j * PAIR, (j + 1) * PAIR)

    with ExitStack() as ctx:
        keep = ctx.enter_context(tc.tile_pool(name="keep", bufs=1))
        work = ctx.enter_context(tc.tile_pool(name="work", bufs=3))
        psum = ctx.enter_context(tc.psum_pool(name="psum", bufs=1))

        def next_bank():
            bank = psum.tile([P, BANK], F32, tag="bank", bufs=8)
            return bank

        ctx.enter_context(tc.manual_schedule())

        ones = keep.tile([P, P], BF16)
        nc.vector.memset(ones[:], 1.0)
        idle_sums = next_bank()
        for n in range(WARM_UP):
            nc.tensor.matmul(out=idle_sums[:, 0:P], lhsT=ones[:], rhs=ones[:], start=True, stop=True)
        bias_rows = keep.tile([P, DIRS, GATES], BF16)
        nc.vector.memset(bias_rows[:].bitcast(I32), 0)
        w_planes = keep.tile([P, DIRS, GATES], U8, align_bytes=64)
        nc.vector.memset(w_planes[:].bitcast(I32), 0)
        ident = keep.tile([P, P], F32)
        make_identity(nc, ident[:])

        warm = keep.tile([P, 1], F32)
        nc.vector.memset(warm[:], 0.0)
        nc.scalar.activation(out=warm[:], in_=warm[:], func=ACT.Sigmoid)

        whh_sb = keep.tile([P, DIRS, HALVES, BANK // P, H], BF16)
        h0_sb = keep.tile([P, DIRS, TILES, H], BF16)
        c0_sb = keep.tile([P, DIRS, TILES, H], BF16)
        gt_sb = keep.tile([P, PASSES, TILES, K_PASS], BF16)
        w_codes = keep.tile([P, DIRS, PASSES, GATES], U32, align_bytes=64)

        def load_hidden(d):
            nc.sync.dma_start(
                out=whh_sb[:, d, :, :, :], in_=whh[d].rearrange("(c p b) k -> p c b k", c=HALVES, p=P)
            )
            nc.sync.dma_start(out=h0_sb[:, d, :, :], in_=by_token(h0[d]))
            nc.sync.dma_start(out=bias_rows[0:1, d, :], in_=bih[d].rearrange("(o n) -> o n", o=1))
            nc.sync.dma_start(out=bias_rows[1:2, d, :], in_=bhh[d].rearrange("(o n) -> o n", o=1))

        def load_gt(j):
            some = pair_tiles(j)
            nc.sync.dma_start(out=gt_sb[:, 0, some, :], in_=by_token(hn_chunks)[:, some, :])
            nc.sync.dma_start(out=gt_sb[:, 1, some, :], in_=by_token(hn_tags)[:, some, :])
            nc.sync.dma_start(out=gt_sb[:, 2, some, 0:X_COLS], in_=by_token(x)[:, some, :])

        def load_wih(d):
            for quadrant in range(4):
                nc.sync.dma_start(
                    out=w_planes[32 * quadrant : 32 * quadrant + 4 * PASSES, d, :].bitcast(I32),
                    in_=wih_scales[d][:, 4 * quadrant : 4 * quadrant + 4, :].bitcast(I32),
                )
            for g in range(PASSES):
                nc.sync.dma_start(
                    out=w_codes[:, d, g, :].bitcast(I32),
                    in_=wih_words[d][g].rearrange("p n t -> p (n t)").bitcast(I32),
                )

        def load_c0(d):
            nc.sync.dma_start(out=c0_sb[:, d, :, :], in_=by_token(c0[d]))

        load_hidden(0)
        nc.sync.dma_start(out=gt_sb[:, 2, :, X_COLS : X_COLS + TAG_COLS], in_=by_token(tags))
        nc.sync.dma_start(out=gt_sb[:, 2, :, X_COLS + TAG_COLS : K_PASS], in_=by_token(chunks))
        load_gt(0)
        load_gt(1)
        load_wih(0)
        load_c0(0)
        load_gt(2)
        load_gt(3)
        load_hidden(1)
        load_wih(1)
        load_c0(1)

        bias = keep.tile([P, DIRS, GATES], F32)
        whh_t = keep.tile([P, DIRS, GATES], F32)
        h0_t = keep.tile([P, DIRS, TILES * P], F32)

        def spread_bias(d):
            for c in range(HALVES):
                spread = next_bank()
                nc.tensor.matmul(out=spread[:], lhsT=ones[:], rhs=bias_rows[:, d, half(c)], start=True, stop=True)
                nc.scalar.copy(out=bias[:, d, half(c)], in_=spread[:])

        def transpose_whh(d):
            for c in range(HALVES):
                turned = next_bank()
                for b in range(BANK // P):
                    nc.tensor.transpose(turned[:, block(b)], whh_sb[:, d, c, b, :].bitcast(F32), ident[:])
                nc.vector.tensor_copy(
                    out=whh_t[:, d, half(c)].rearrange("j (p b) -> j p b", p=P),
                    in_=turned[:].rearrange("j (b p) -> j p b", p=P),
                )

        def transpose_h0(d):
            for c in range(TILES * P // BANK):
                turned = next_bank()
                for b in range(BANK // P):
                    nc.tensor.transpose(turned[:, block(b)], h0_sb[:, d, c * (BANK // P) + b, :].bitcast(F32), ident[:])
                nc.scalar.copy(out=h0_t[:, d, half(c)], in_=turned[:])

        gt_codes = keep.tile([P, PASSES, TILES * P], U32, align_bytes=64)
        gt_scales = keep.tile([P, PASSES, TILES * P], U8, align_bytes=64)

        def sort_gt(j):
            halves = work.tile([P, PASSES, PAIR, 2, P], F32, tag="halves")
            for g in range(PASSES):
                nc.scalar.copy(
                    out=halves[:, g, :, :, :],
                    in_=gt_sb[:, g, pair_tiles(j), :].bitcast(F32).rearrange("p t (c w) -> p t w c", w=2),
                )
            return halves

        def transpose_gt(halves):
            grouped = work.tile([P, PASSES, PAIR * P * 4], BF16, tag="grouped", align_bytes=64)
            for g in range(PASSES):
                turned = next_bank()
                for t in range(PAIR):
                    for w in range(2):
                        nc.tensor.transpose(turned[:, block(2 * t + w)], halves[:, g, t, w, :], ident[:])
                nc.scalar.copy(
                    out=grouped[:, g, :].bitcast(F32).rearrange("p (t c w) -> p t c w", t=PAIR, w=2),
                    in_=turned[:].rearrange("p (t w c) -> p t c w", t=PAIR, w=2),
                )
            return grouped

        def quantise_gt(j, grouped):
            cols = slice(j * PAIR * P, (j + 1) * PAIR * P)
            for g in range(PASSES):
                nc.vector.quantize_mx(
                    out=gt_codes[:, g, cols].bitcast(FP8X4), scales=gt_scales[:, g, cols], in_=grouped[:, g, :]
                )

        def hidden_product(d, j):
            gates = work.tile([P, PAIR, GATES], F32, tag="gates", bufs=5)
            for t in range(PAIR):
                for c in range(HALVES):
                    sums = next_bank()
                    for e in range(2):
                        nc.tensor.matmul(
                            out=sums[:],
                            lhsT=h0_t[:, d, block(j * PAIR + t)].bitcast(BF16)[:, e : 2 * P : 2],
                            rhs=whh_t[:, d, half(c)].bitcast(BF16)[:, e : 2 * BANK : 2],
                            start=(e == 0),
                            stop=(e == 1),
                        )
                    nc.vector.tensor_tensor(out=gates[:, t, half(c)], in0=sums[:], in1=bias[:, d, half(c)], op=ALU.add)
            return gates

        def input_columns(d, j, gates, t, cols):
            sums = next_bank()
            width = cols.stop - cols.start
            for g in range(PASSES):
                nc.tensor.matmul_mx(
                    out=sums[:, 0:width],
                    lhsT=gt_codes[:, g, block(j * PAIR + t)].bitcast(FP8X4),
                    lhsT_scale=gt_scales[:, g, block(j * PAIR + t)],
                    rhs=w_codes[:, d, g, cols].bitcast(FP8X4),
                    rhs_scale=w_planes[4 * g : P, d, cols],
                    start=(g == 0),
                    stop=(g == PASSES - 1),
                )
            nc.vector.tensor_tensor(out=gates[:, t, cols], in0=sums[:, 0:width], in1=gates[:, t, cols], op=ALU.add)

        def input_product(d, j, gates):
            for c in range(HALVES):
                for t in range(PAIR):
                    input_columns(d, j, gates, t, half(c))

        def gate(gates, some, q, func):
            nc.scalar.activation(
                out=gates[:, some, q.start * H : q.stop * H], in_=gates[:, some, q.start * H : q.stop * H], func=func
            )

        def count(some):
            return some.stop - some.start

        def keep_old(engine, u, gates, some):
            d, j = divmod(u, PAIRS)
            kept = work.tile([P, count(some), H], F32, tag="kept", bufs=4)
            engine.tensor_tensor(
                out=kept[:],
                in0=gates[:, some, H : 2 * H],
                in1=c0_sb[:, d, j * PAIR + some.start : j * PAIR + some.stop, :],
                op=ALU.mult,
            )
            return kept

        def take_new(engine, gates, some):
            state = work.tile([P, count(some), H], F32, tag="state", bufs=4)
            engine.tensor_tensor(out=state[:], in0=gates[:, some, 0:H], in1=gates[:, some, 2 * H : 3 * H], op=ALU.mult)
            return state

        def join(engine, state, kept):
            engine.tensor_tensor(out=state[:], in0=state[:], in1=kept[:], op=ALU.add)

        def squash(state):
            nc.scalar.activation(out=state[:], in_=state[:], func=ACT.Tanh)

        def emit(engine, u, gates, some, state):
            d, j = divmod(u, PAIRS)
            hidden = work.tile([P, count(some), H], F32, tag="hidden", bufs=4)
            engine.tensor_tensor(out=hidden[:], in0=gates[:, some, 3 * H : 4 * H], in1=state[:], op=ALU.mult)
            nc.sync.dma_start(
                out=by_token(out)[:, j * PAIR + some.start : j * PAIR + some.stop, d * H : (d + 1) * H], in_=hidden[:]
            )

        I_F, GG, O = slice(0, 2), slice(2, 3), slice(3, 4)
        BOTH, FIRST, SECOND = slice(0, 2), slice(0, 1), slice(1, 2)

        def cell_start(u, gates):
            gate(gates, BOTH, I_F, ACT.Sigmoid)
            kept = keep_old(nc.gpsimd, u, gates, BOTH)
            gate(gates, BOTH, GG, ACT.Tanh)
            state = take_new(nc.gpsimd, gates, BOTH)
            join(nc.gpsimd, state, kept)
            gate(gates, BOTH, O, ACT.Sigmoid)
            return state

        def cell_end(u, gates, state):
            squash(state)
            emit(nc.gpsimd, u, gates, BOTH, state)

        def prepare(d):
            transpose_whh(d)
            transpose_h0(d)
            spread_bias(d)

        prepare(0)
        sorted_of = {0: sort_gt(0)}
        gates_of = {}
        grouped_of = {}
        state_of = {}
        gates_of[0] = hidden_product(0, 0)
        for u in range(UNITS - 1):
            if u == PAIRS - 1:
                prepare(1)
            if 0 <= u - 1 < PAIRS:
                quantise_gt(u - 1, grouped_of[u - 1])
            if u + 1 < PAIRS:
                gates_of[u + 1] = hidden_product(0, u + 1)
            if PAIRS <= u:
                gates_of[u] = hidden_product(u // PAIRS, u % PAIRS)
            if u < PAIRS:
                grouped_of[u] = transpose_gt(sorted_of[u])
            if u + 1 < PAIRS:
                sorted_of[u + 1] = sort_gt(u + 1)
            if 0 <= u - 1:
                input_product((u - 1) // PAIRS, (u - 1) % PAIRS, gates_of[u - 1])
                state_of[u - 1] = cell_start(u - 1, gates_of[u - 1])
            if 0 <= u - 2:
                cell_end(u - 2, gates_of[u - 2], state_of[u - 2])

        last = UNITS - 1
        d_last, j_last = divmod(last, PAIRS)
        before = gates_of[last - 1]
        input_product(d_last, j_last - 1, before)
        gate(before, BOTH, I_F, ACT.Sigmoid)
        kept_before = keep_old(nc.gpsimd, last - 1, before, BOTH)
        gate(before, BOTH, GG, ACT.Tanh)
        state_before = take_new(nc.gpsimd, before, BOTH)
        gate(before, BOTH, O, ACT.Sigmoid)
        squash(state_of[last - 2])
        gates = hidden_product(d_last, j_last)
        input_columns(d_last, j_last, gates, 0, half(0))
        input_columns(d_last, j_last, gates, 0, half(1))
        input_columns(d_last, j_last, gates, 1, half(0))
        input_columns(d_last, j_last, gates, 1, slice(2 * H, 3 * H))
        input_columns(d_last, j_last, gates, 1, slice(3 * H, 4 * H))
        gate(gates, FIRST, I_F, ACT.Sigmoid)
        gate(gates, FIRST, GG, ACT.Tanh)
        gate(gates, FIRST, O, ACT.Sigmoid)
        gate(gates, SECOND, I_F, ACT.Sigmoid)
        gate(gates, SECOND, GG, ACT.Tanh)
        emit(nc.vector, last - 2, gates_of[last - 2], BOTH, state_of[last - 2])
        join(nc.vector, state_before, kept_before)
        squash(state_before)
        kept_first = keep_old(nc.vector, last, gates, FIRST)
        state_first = take_new(nc.vector, gates, FIRST)
        join(nc.vector, state_first, kept_first)
        squash(state_first)
        kept_second = keep_old(nc.vector, last, gates, SECOND)
        state_second = take_new(nc.vector, gates, SECOND)
        join(nc.vector, state_second, kept_second)
        gate(gates, SECOND, O, ACT.Sigmoid)
        squash(state_second)
        emit(nc.vector, last - 1, before, BOTH, state_before)
        emit(nc.vector, last, gates, FIRST, state_first)
        emit(nc.vector, last, gates, SECOND, state_second)
